import numpy as np
import ml_dtypes


def mxq(x, axis, fmt="e4m3"):
    dtype, down = {"e4m3": (ml_dtypes.float8_e4m3fn, 7), "e5m2": (ml_dtypes.float8_e5m2, 14)}[fmt]
    v = np.moveaxis(np.asarray(x, np.float32).astype(ml_dtypes.bfloat16).astype(np.float64), axis, -1)
    blocks = v.reshape(v.shape[:-1] + (-1, 32))
    amax = np.abs(blocks).max(-1, keepdims=True)
    byte = np.maximum(np.where(amax > 0, np.frexp(amax)[1] - 1 + 127, 0) - down, 1)
    scale = np.exp2(byte - 127.0)
    codes = (blocks / scale).astype(np.float32).astype(dtype).astype(np.float64)
    return np.moveaxis((codes * scale).reshape(v.shape), -1, axis)


WIDE = False


def mx_kscale(k):
    if not WIDE:
        return np.ones(k)
    levels = np.array([10, -10, 5, -5, 0])
    a = np.random.permutation(np.resize(levels, k // 512 * 4)).reshape(k // 512, 4)
    idx = np.arange(k)
    return np.exp2(a[idx // 512, idx % 128 // 32])


BF16 = ml_dtypes.bfloat16


def bf(x):
    return np.asarray(x, np.float32).astype(BF16)


def f64(x):
    return np.asarray(x).astype(np.float64)


E2M1 = np.array([0.0, 0.5, 1.0, 1.5, 2.0, 3.0, 4.0, 6.0, -0.0, -0.5, -1.0, -1.5, -2.0, -3.0, -4.0, -6.0])


def pack_weight(w, fmt):
    k, n = w.shape
    w = f64(bf(w)).reshape(k // 32, 32, n)
    amax = np.abs(w).max(1)
    if fmt == "e4m3":
        byte = np.frexp(amax)[1] - 1 + 127 - 7
    else:
        mant, ex = np.frexp(amax / 6.0)
        byte = np.where(mant > 0.5, ex, ex - 1) + 127
    byte = np.clip(np.where(amax > 0, byte, 1), 1, 254)
    scaled = (w * np.exp2(127.0 - byte)[:, None, :]).reshape(k, n).astype(np.float32)
    by_word = np.ascontiguousarray(scaled.reshape(k // 512, 128, 4, n).transpose(0, 1, 3, 2))
    if fmt == "e4m3":
        words = by_word.astype(ml_dtypes.float8_e4m3fn).view(np.uint8)
    else:
        c = by_word.astype(ml_dtypes.float4_e2m1fn).view(np.uint8) & 0xF
        words = c[..., 0::2] | (c[..., 1::2] << 4)
    return np.ascontiguousarray(words), np.ascontiguousarray(byte.astype(np.uint8).reshape(k // 512, 16, n))


def unpack_weight(words, scales, fmt):
    g, p, n, _ = words.shape
    if fmt == "e4m3":
        vals = np.ascontiguousarray(words).view(ml_dtypes.float8_e4m3fn).astype(np.float64)
    else:
        nib = np.empty((g, p, n, 4), np.uint8)
        nib[..., 0::2] = words & 0xF
        nib[..., 1::2] = words >> 4
        vals = E2M1[nib]
    vals = vals * np.repeat(np.exp2(scales.astype(np.float64) - 127.0), 8, axis=1)[..., None]
    return vals.transpose(0, 1, 3, 2).reshape(g * 512, n)

def pack4(w):
    words, scales = pack_weight(w, "e2m1")
    return words.reshape(words.shape[0], 128, -1), scales


def unpack4(words, scales):
    return unpack_weight(words.reshape(words.shape[0], 128, -1, 2), scales, "e2m1")


B, S, H = 8, 65, 512
N = B * (S - 1)
G = 0.75


def setup_inputs():
    s = mx_kscale(H)
    x = bf(np.random.standard_normal((B, S, H)) * s)
    k1 = bf(np.random.standard_normal((N, H)) * G * s)
    k2 = bf(np.random.standard_normal((N, H)) * G * np.sqrt(1.0 + 0.25 * G * G) * s)
    coefficients = np.random.standard_normal((H, H)) * G / np.sqrt(H) * s[:, None] / s[None, :]
    words, scales = pack4(np.ascontiguousarray(coefficients.T))
    return {"x": x,
            "k1": k1,
            "k2": k2,
            "coefficients_words": words,
            "coefficients_scales": scales}


def reference(x, k1, k2, coefficients_words, coefficients_scales):
    x, k1, k2 = f64(x), f64(k1), f64(k2)
    y = x[:, :-1, :].reshape(-1, H)
    ct = unpack4(coefficients_words, coefficients_scales)
    k3 = mxq(y + 0.5 * k2, 1, "e4m3") @ ct
    k4 = mxq(y + k3, 1, "e4m3") @ ct
    y1 = y + (k1 + 2.0 * k2 + 2.0 * k3 + k4) / 6.0
    return y1.reshape(B, S - 1, H) - x[:, 1:, :]

@@ -1,0 +1,158 @@
+from contextlib import ExitStack
+
+import concourse.mybir as mybir
+from concourse.masks import make_identity
+
+F32 = mybir.dt.float32
+BF16 = mybir.dt.bfloat16
+I32 = mybir.dt.int32
+U32 = mybir.dt.uint32
+U8 = mybir.dt.uint8
+FP8X4 = mybir.dt.float8_e4m3fn_x4
+FP4X4 = mybir.dt.float4_e2m1fn_x4
+ADD = mybir.AluOpType.add
+SUBTRACT = mybir.AluOpType.subtract
+MULT = mybir.AluOpType.mult
+
+P = 128
+H = 512
+SEQS = 8
+STEPS = 64
+GROUPS = 4
+WORDS = H // 2
+
+FLOPS = 2 * 2 * SEQS * STEPS * H * H
+
+
+def tile_sindylossmixin_pa_s_kernel(
+    tc, x, k1, k2, coefficients_words, coefficients_scales, out
+):
+    nc = tc.nc
+
+    y_dram = x[:, 0:STEPS, :].rearrange("b (q g) h -> q b g h", g=GROUPS)
+    next_dram = x[:, 1 : STEPS + 1, :].rearrange("b (q g) h -> q b g h", g=GROUPS)
+    k1_dram = k1.rearrange("(b q g) h -> q b g h", b=SEQS, g=GROUPS)
+    k2_dram = k2.rearrange("(b q g) h -> q b g h", b=SEQS, g=GROUPS)
+    out_dram = out.rearrange("b (q g) h -> q b g h", g=GROUPS)
+
+    with ExitStack() as ctx:
+        keep = ctx.enter_context(tc.tile_pool(name="keep", bufs=1))
+        psum = ctx.enter_context(tc.psum_pool(name="psum", bufs=GROUPS))
+
+        y_sb = keep.tile([P, GROUPS, H], BF16)
+        k1_sb = keep.tile([P, GROUPS, H], BF16)
+        k2_sb = keep.tile([P, GROUPS, H], BF16)
+        next_sb = keep.tile([P, GROUPS, H], BF16)
+        w_words = keep.tile([P, 2 * H], U8, align_bytes=64)
+        w_scales = keep.tile([P, H], U8, align_bytes=64)
+
+        nc.vector.memset(w_scales[:].bitcast(I32), 0)
+        ident = keep.tile([P, P], F32)
+        make_identity(nc, ident[:])
+
+        for g in range(2):
+            nc.sync.dma_start(out=y_sb[:, g, :], in_=y_dram[:, :, g, :])
+            nc.sync.dma_start(out=k2_sb[:, g, :], in_=k2_dram[:, :, g, :])
+        nc.sync.dma_start(out=w_words[:].bitcast(I32), in_=coefficients_words[0].bitcast(I32))
+        for quadrant in range(4):
+            nc.sync.dma_start(
+                out=w_scales[32 * quadrant : 32 * quadrant + 4, :].bitcast(I32),
+                in_=coefficients_scales[0, 4 * quadrant : 4 * quadrant + 4, :].bitcast(I32),
+            )
+        nc.sync.dma_start(out=y_sb[:, 2:GROUPS, :], in_=y_dram[:, :, 2:GROUPS, :])
+        nc.sync.dma_start(out=k2_sb[:, 2:GROUPS, :], in_=k2_dram[:, :, 2:GROUPS, :])
+        nc.sync.dma_start(out=k1_sb[:], in_=k1_dram)
+        nc.sync.dma_start(out=next_sb[:], in_=next_dram)
+
+        stage_in = keep.tile([P, 2, GROUPS, H], BF16)
+        grouped = keep.tile([P, 2, GROUPS, P, 2], F32, align_bytes=64)
+        codes = keep.tile([P, 2, GROUPS, P], U32, align_bytes=64)
+        scales = keep.tile([P, 2, GROUPS, P], U8, align_bytes=64)
+        base = keep.tile([P, GROUPS, H], F32)
+        result = keep.tile([P, GROUPS, H], F32)
+
+        def quantise_group(stage, g, bank):
+            words = stage_in[:, stage, g, :].bitcast(F32)
+            for u in range(2):
+                nc.tensor.transpose(bank[:, u, :], words[:, u:WORDS:2], ident[:])
+            nc.scalar.copy(out=grouped[:, stage, g, :, :], in_=bank.rearrange("p u r -> p r u"))
+            nc.vector.quantize_mx(
+                out=codes[:, stage, g, :].bitcast(FP8X4),
+                scales=scales[:, stage, g, :],
+                in_=grouped[:, stage, g, :, :].rearrange("p r u -> p (r u)").bitcast(BF16),
+            )
+
+        def times_w(acc, stage, g, start, stop):
+            nc.tensor.matmul_mx(
+                out=acc[:],
+                lhsT=codes[:, stage, g, :].bitcast(FP8X4),
+                lhsT_scale=scales[:, stage, g, :],
+                rhs=w_words[:].bitcast(FP4X4),
+                rhs_scale=w_scales[:],
+                start=start,
+                stop=stop,
+            )
+
+        for g in range(GROUPS):
+            nc.vector.scalar_tensor_tensor(
+                out=stage_in[:, 0, g, :],
+                in0=k2_sb[:, g, :],
+                scalar=0.5,
+                in1=y_sb[:, g, :],
+                op0=MULT,
+                op1=ADD,
+            )
+        k3_banks = []
+        for g in range(GROUPS):
+            turned = psum.tile([P, 2, P], F32, tag="first")
+            quantise_group(0, g, turned)
+            k3 = psum.tile([P, H], F32, tag="second")
+            times_w(k3, 0, g, True, True)
+            k3_banks.append(k3)
+
+        sums = []
+        for g in range(GROUPS):
+            nc.vector.tensor_tensor(
+                out=stage_in[:, 1, g, :], in0=k3_banks[g][:], in1=y_sb[:, g, :], op=ADD
+            )
+            turned = psum.tile([P, 2, P], F32, tag="second")
+            quantise_group(1, g, turned)
+            total = psum.tile([P, H], F32, tag="first")
+            times_w(total, 0, g, True, False)
+            times_w(total, 0, g, False, False)
+            times_w(total, 1, g, False, True)
+            sums.append(total)
+
+        for g in range(GROUPS):
+            nc.vector.scalar_tensor_tensor(
+                out=base[:, g, :],
+                in0=k2_sb[:, g, :],
+                scalar=1.0 / 3.0,
+                in1=y_sb[:, g, :],
+                op0=MULT,
+                op1=ADD,
+            )
+        for g in range(GROUPS):
+            nc.vector.scalar_tensor_tensor(
+                out=base[:, g, :],
+                in0=k1_sb[:, g, :],
+                scalar=1.0 / 6.0,
+                in1=base[:, g, :],
+                op0=MULT,
+                op1=ADD,
+            )
+        for g in range(GROUPS):
+            nc.vector.tensor_tensor(
+                out=base[:, g, :], in0=base[:, g, :], in1=next_sb[:, g, :], op=SUBTRACT
+            )
+
+        for g in range(GROUPS):
+            nc.vector.scalar_tensor_tensor(
+                out=result[:, g, :],
+                in0=sums[g][:],
+                scalar=1.0 / 6.0,
+                in1=base[:, g, :],
+                op0=MULT,
+                op1=ADD,
+            )
+            nc.sync.dma_start(out=out_dram[:, :, g, :], in_=result[:, g, :])

@@ -11,7 +11,6 @@ U8 = mybir.dt.uint8
 FP8X4 = mybir.dt.float8_e4m3fn_x4
 FP4X4 = mybir.dt.float4_e2m1fn_x4
 ADD = mybir.AluOpType.add
-SUBTRACT = mybir.AluOpType.subtract
 MULT = mybir.AluOpType.mult
 
 P = 128
@@ -61,8 +60,8 @@ def tile_sindylossmixin_pa_s_kernel(
             )
         nc.sync.dma_start(out=y_sb[:, 2:GROUPS, :], in_=y_dram[:, :, 2:GROUPS, :])
         nc.sync.dma_start(out=k2_sb[:, 2:GROUPS, :], in_=k2_dram[:, :, 2:GROUPS, :])
-        nc.sync.dma_start(out=k1_sb[:], in_=k1_dram)
         nc.sync.dma_start(out=next_sb[:], in_=next_dram)
+        nc.sync.dma_start(out=k1_sb[:], in_=k1_dram)
 
         stage_in = keep.tile([P, 2, GROUPS, H], BF16)
         grouped = keep.tile([P, 2, GROUPS, P, 2], F32, align_bytes=64)
@@ -71,11 +70,13 @@ def tile_sindylossmixin_pa_s_kernel(
         base = keep.tile([P, GROUPS, H], F32)
         result = keep.tile([P, GROUPS, H], F32)
 
-        def quantise_group(stage, g, bank):
+        def turn_group(stage, g, bank):
             words = stage_in[:, stage, g, :].bitcast(F32)
             for u in range(2):
                 nc.tensor.transpose(bank[:, u, :], words[:, u:WORDS:2], ident[:])
             nc.scalar.copy(out=grouped[:, stage, g, :, :], in_=bank.rearrange("p u r -> p r u"))
+
+        def quantise_group(stage, g):
             nc.vector.quantize_mx(
                 out=codes[:, stage, g, :].bitcast(FP8X4),
                 scales=scales[:, stage, g, :],
@@ -93,6 +94,18 @@ def tile_sindylossmixin_pa_s_kernel(
                 stop=stop,
             )
 
+        def base_step(g, in0, scalar):
+            nc.vector.scalar_tensor_tensor(
+                out=base[:, g, :],
+                in0=in0[:, g, :],
+                scalar=scalar,
+                in1=base[:, g, :],
+                op0=MULT,
+                op1=ADD,
+            )
+
+        ctx.enter_context(tc.manual_schedule())
+
         for g in range(GROUPS):
             nc.vector.scalar_tensor_tensor(
                 out=stage_in[:, 0, g, :],
@@ -102,27 +115,11 @@ def tile_sindylossmixin_pa_s_kernel(
                 op0=MULT,
                 op1=ADD,
             )
-        k3_banks = []
-        for g in range(GROUPS):
             turned = psum.tile([P, 2, P], F32, tag="first")
-            quantise_group(0, g, turned)
-            k3 = psum.tile([P, H], F32, tag="second")
-            times_w(k3, 0, g, True, True)
-            k3_banks.append(k3)
+            turn_group(0, g, turned)
 
+        k3_banks = []
         sums = []
-        for g in range(GROUPS):
-            nc.vector.tensor_tensor(
-                out=stage_in[:, 1, g, :], in0=k3_banks[g][:], in1=y_sb[:, g, :], op=ADD
-            )
-            turned = psum.tile([P, 2, P], F32, tag="second")
-            quantise_group(1, g, turned)
-            total = psum.tile([P, H], F32, tag="first")
-            times_w(total, 0, g, True, False)
-            times_w(total, 0, g, False, False)
-            times_w(total, 1, g, False, True)
-            sums.append(total)
-
         for g in range(GROUPS):
             nc.vector.scalar_tensor_tensor(
                 out=base[:, g, :],
@@ -132,19 +129,27 @@ def tile_sindylossmixin_pa_s_kernel(
                 op0=MULT,
                 op1=ADD,
             )
-        for g in range(GROUPS):
-            nc.vector.scalar_tensor_tensor(
-                out=base[:, g, :],
-                in0=k1_sb[:, g, :],
-                scalar=1.0 / 6.0,
-                in1=base[:, g, :],
-                op0=MULT,
-                op1=ADD,
-            )
+            quantise_group(0, g)
+            k3 = psum.tile([P, H], F32, tag="second")
+            times_w(k3, 0, g, True, True)
+            k3_banks.append(k3)
+            total = psum.tile([P, H], F32, tag="first")
+            times_w(total, 0, g, True, False)
+            times_w(total, 0, g, False, False)
+            sums.append(total)
+
         for g in range(GROUPS):
             nc.vector.tensor_tensor(
-                out=base[:, g, :], in0=base[:, g, :], in1=next_sb[:, g, :], op=SUBTRACT
+                out=stage_in[:, 1, g, :], in0=k3_banks[g][:], in1=y_sb[:, g, :], op=ADD
             )
+            turned = psum.tile([P, 2, P], F32, tag="second")
+            turn_group(1, g, turned)
+            base_step(g, next_sb, -1.0)
+
+        for g in range(GROUPS):
+            base_step(g, k1_sb, 1.0 / 6.0)
+            quantise_group(1, g)
+            times_w(sums[g], 1, g, False, True)
 
         for g in range(GROUPS):
             nc.vector.scalar_tensor_tensor(

@@ -52,17 +52,18 @@ def tile_sindylossmixin_pa_s_kernel(
         for g in range(2):
             nc.sync.dma_start(out=y_sb[:, g, :], in_=y_dram[:, :, g, :])
             nc.sync.dma_start(out=k2_sb[:, g, :], in_=k2_dram[:, :, g, :])
+        nc.sync.dma_start(out=y_sb[:, 2:GROUPS, :], in_=y_dram[:, :, 2:GROUPS, :])
+        nc.sync.dma_start(out=k2_sb[:, 2:GROUPS, :], in_=k2_dram[:, :, 2:GROUPS, :])
         nc.sync.dma_start(out=w_words[:].bitcast(I32), in_=coefficients_words[0].bitcast(I32))
         for quadrant in range(4):
             nc.sync.dma_start(
                 out=w_scales[32 * quadrant : 32 * quadrant + 4, :].bitcast(I32),
                 in_=coefficients_scales[0, 4 * quadrant : 4 * quadrant + 4, :].bitcast(I32),
             )
-        nc.sync.dma_start(out=y_sb[:, 2:GROUPS, :], in_=y_dram[:, :, 2:GROUPS, :])
-        nc.sync.dma_start(out=k2_sb[:, 2:GROUPS, :], in_=k2_dram[:, :, 2:GROUPS, :])
         nc.sync.dma_start(out=next_sb[:], in_=next_dram)
         nc.sync.dma_start(out=k1_sb[:], in_=k1_dram)
 
+        half_k2 = keep.tile([P, GROUPS, H], BF16)
         stage_in = keep.tile([P, 2, GROUPS, H], BF16)
         grouped = keep.tile([P, 2, GROUPS, P, 2], F32, align_bytes=64)
         codes = keep.tile([P, 2, GROUPS, P], U32, align_bytes=64)
@@ -107,19 +108,8 @@ def tile_sindylossmixin_pa_s_kernel(
         ctx.enter_context(tc.manual_schedule())
 
         for g in range(GROUPS):
-            nc.vector.scalar_tensor_tensor(
-                out=stage_in[:, 0, g, :],
-                in0=k2_sb[:, g, :],
-                scalar=0.5,
-                in1=y_sb[:, g, :],
-                op0=MULT,
-                op1=ADD,
-            )
-            turned = psum.tile([P, 2, P], F32, tag="first")
-            turn_group(0, g, turned)
+            nc.scalar.mul(out=half_k2[:, g, :], in_=k2_sb[:, g, :], mul=0.5)
 
-        k3_banks = []
-        sums = []
         for g in range(GROUPS):
             nc.vector.scalar_tensor_tensor(
                 out=base[:, g, :],
@@ -129,6 +119,16 @@ def tile_sindylossmixin_pa_s_kernel(
                 op0=MULT,
                 op1=ADD,
             )
+            nc.vector.tensor_tensor(
+                out=stage_in[:, 0, g, :], in0=y_sb[:, g, :], in1=half_k2[:, g, :], op=ADD
+            )
+            turned = psum.tile([P, 2, P], F32, tag="first")
+            turn_group(0, g, turned)
+
+        k3_banks = []
+        sums = []
+        for g in range(GROUPS):
+            base_step(g, next_sb, -1.0)
             quantise_group(0, g)
             k3 = psum.tile([P, H], F32, tag="second")
             times_w(k3, 0, g, True, True)
@@ -144,7 +144,6 @@ def tile_sindylossmixin_pa_s_kernel(
             )
             turned = psum.tile([P, 2, P], F32, tag="second")
             turn_group(1, g, turned)
-            base_step(g, next_sb, -1.0)
 
         for g in range(GROUPS):
             base_step(g, k1_sb, 1.0 / 6.0)

@@ -50,18 +50,20 @@ def tile_sindylossmixin_pa_s_kernel(
         make_identity(nc, ident[:])
 
         for g in range(2):
-            nc.sync.dma_start(out=y_sb[:, g, :], in_=y_dram[:, :, g, :])
             nc.sync.dma_start(out=k2_sb[:, g, :], in_=k2_dram[:, :, g, :])
-        nc.sync.dma_start(out=y_sb[:, 2:GROUPS, :], in_=y_dram[:, :, 2:GROUPS, :])
+            nc.sync.dma_start(out=y_sb[:, g, :], in_=y_dram[:, :, g, :])
         nc.sync.dma_start(out=k2_sb[:, 2:GROUPS, :], in_=k2_dram[:, :, 2:GROUPS, :])
+        nc.sync.dma_start(out=y_sb[:, 2:GROUPS, :], in_=y_dram[:, :, 2:GROUPS, :])
         nc.sync.dma_start(out=w_words[:].bitcast(I32), in_=coefficients_words[0].bitcast(I32))
         for quadrant in range(4):
             nc.sync.dma_start(
                 out=w_scales[32 * quadrant : 32 * quadrant + 4, :].bitcast(I32),
                 in_=coefficients_scales[0, 4 * quadrant : 4 * quadrant + 4, :].bitcast(I32),
             )
-        nc.sync.dma_start(out=next_sb[:], in_=next_dram)
-        nc.sync.dma_start(out=k1_sb[:], in_=k1_dram)
+        for half in (slice(0, GROUPS // 2), slice(GROUPS // 2, GROUPS)):
+            nc.sync.dma_start(out=next_sb[:, half, :], in_=next_dram[:, :, half, :])
+        for half in (slice(0, GROUPS // 2), slice(GROUPS // 2, GROUPS)):
+            nc.sync.dma_start(out=k1_sb[:, half, :], in_=k1_dram[:, :, half, :])
 
         half_k2 = keep.tile([P, GROUPS, H], BF16)
         stage_in = keep.tile([P, 2, GROUPS, H], BF16)
@@ -135,7 +137,6 @@ def tile_sindylossmixin_pa_s_kernel(
             k3_banks.append(k3)
             total = psum.tile([P, H], F32, tag="first")
             times_w(total, 0, g, True, False)
-            times_w(total, 0, g, False, False)
             sums.append(total)
 
         for g in range(GROUPS):
@@ -147,6 +148,7 @@ def tile_sindylossmixin_pa_s_kernel(
 
         for g in range(GROUPS):
             base_step(g, k1_sb, 1.0 / 6.0)
+            times_w(sums[g], 0, g, False, False)
             quantise_group(1, g)
             times_w(sums[g], 1, g, False, True)
 

@@ -11,6 +11,7 @@ U8 = mybir.dt.uint8
 FP8X4 = mybir.dt.float8_e4m3fn_x4
 FP4X4 = mybir.dt.float4_e2m1fn_x4
 ADD = mybir.AluOpType.add
+SUBTRACT = mybir.AluOpType.subtract
 MULT = mybir.AluOpType.mult
 
 P = 128
@@ -49,11 +50,9 @@ def tile_sindylossmixin_pa_s_kernel(
         ident = keep.tile([P, P], F32)
         make_identity(nc, ident[:])
 
-        for g in range(2):
+        for g in range(GROUPS):
             nc.sync.dma_start(out=k2_sb[:, g, :], in_=k2_dram[:, :, g, :])
             nc.sync.dma_start(out=y_sb[:, g, :], in_=y_dram[:, :, g, :])
-        nc.sync.dma_start(out=k2_sb[:, 2:GROUPS, :], in_=k2_dram[:, :, 2:GROUPS, :])
-        nc.sync.dma_start(out=y_sb[:, 2:GROUPS, :], in_=y_dram[:, :, 2:GROUPS, :])
         nc.sync.dma_start(out=w_words[:].bitcast(I32), in_=coefficients_words[0].bitcast(I32))
         for quadrant in range(4):
             nc.sync.dma_start(
@@ -61,9 +60,9 @@ def tile_sindylossmixin_pa_s_kernel(
                 in_=coefficients_scales[0, 4 * quadrant : 4 * quadrant + 4, :].bitcast(I32),
             )
         for half in (slice(0, GROUPS // 2), slice(GROUPS // 2, GROUPS)):
-            nc.sync.dma_start(out=next_sb[:, half, :], in_=next_dram[:, :, half, :])
-        for half in (slice(0, GROUPS // 2), slice(GROUPS // 2, GROUPS)):
             nc.sync.dma_start(out=k1_sb[:, half, :], in_=k1_dram[:, :, half, :])
+        for half in (slice(0, GROUPS // 2), slice(GROUPS // 2, GROUPS)):
+            nc.sync.dma_start(out=next_sb[:, half, :], in_=next_dram[:, :, half, :])
 
         half_k2 = keep.tile([P, GROUPS, H], BF16)
         stage_in = keep.tile([P, 2, GROUPS, H], BF16)
@@ -130,7 +129,7 @@ def tile_sindylossmixin_pa_s_kernel(
         k3_banks = []
         sums = []
         for g in range(GROUPS):
-            base_step(g, next_sb, -1.0)
+            base_step(g, k1_sb, 1.0 / 6.0)
             quantise_group(0, g)
             k3 = psum.tile([P, H], F32, tag="second")
             times_w(k3, 0, g, True, True)
@@ -138,6 +137,11 @@ def tile_sindylossmixin_pa_s_kernel(
             total = psum.tile([P, H], F32, tag="first")
             times_w(total, 0, g, True, False)
             sums.append(total)
+
+        for g in reversed(range(GROUPS // 2, GROUPS)):
+            nc.gpsimd.tensor_tensor(
+                out=base[:, g, :], in0=base[:, g, :], in1=next_sb[:, g, :], op=SUBTRACT
+            )
 
         for g in range(GROUPS):
             nc.vector.tensor_tensor(
@@ -147,7 +151,8 @@ def tile_sindylossmixin_pa_s_kernel(
             turn_group(1, g, turned)
 
         for g in range(GROUPS):
-            base_step(g, k1_sb, 1.0 / 6.0)
+            if g < GROUPS // 2:
+                base_step(g, next_sb, -1.0)
             times_w(sums[g], 0, g, False, False)
             quantise_group(1, g)
             times_w(sums[g], 1, g, False, True)

@@ -11,7 +11,6 @@ U8 = mybir.dt.uint8
 FP8X4 = mybir.dt.float8_e4m3fn_x4
 FP4X4 = mybir.dt.float4_e2m1fn_x4
 ADD = mybir.AluOpType.add
-SUBTRACT = mybir.AluOpType.subtract
 MULT = mybir.AluOpType.mult
 
 P = 128
@@ -138,11 +137,6 @@ def tile_sindylossmixin_pa_s_kernel(
             times_w(total, 0, g, True, False)
             sums.append(total)
 
-        for g in reversed(range(GROUPS // 2, GROUPS)):
-            nc.gpsimd.tensor_tensor(
-                out=base[:, g, :], in0=base[:, g, :], in1=next_sb[:, g, :], op=SUBTRACT
-            )
-
         for g in range(GROUPS):
             nc.vector.tensor_tensor(
                 out=stage_in[:, 1, g, :], in0=k3_banks[g][:], in1=y_sb[:, g, :], op=ADD
@@ -151,8 +145,7 @@ def tile_sindylossmixin_pa_s_kernel(
             turn_group(1, g, turned)
 
         for g in range(GROUPS):
-            if g < GROUPS // 2:
-                base_step(g, next_sb, -1.0)
+            base_step(g, next_sb, -1.0)
             times_w(sums[g], 0, g, False, False)
             quantise_group(1, g)
             times_w(sums[g], 1, g, False, True)

@@ -11,6 +11,7 @@ U8 = mybir.dt.uint8
 FP8X4 = mybir.dt.float8_e4m3fn_x4
 FP4X4 = mybir.dt.float4_e2m1fn_x4
 ADD = mybir.AluOpType.add
+SUBTRACT = mybir.AluOpType.subtract
 MULT = mybir.AluOpType.mult
 
 P = 128
@@ -18,7 +19,13 @@ H = 512
 SEQS = 8
 STEPS = 64
 GROUPS = 4
+STAGES = 2
+PAIRS = 2
 WORDS = H // 2
+QUADRANTS = 4
+QUADRANT = 32
+LIVE_ROWS = 4
+MX_ALIGN = 64
 
 FLOPS = 2 * 2 * SEQS * STEPS * H * H
 
@@ -42,8 +49,8 @@ def tile_sindylossmixin_pa_s_kernel(
         k1_sb = keep.tile([P, GROUPS, H], BF16)
         k2_sb = keep.tile([P, GROUPS, H], BF16)
         next_sb = keep.tile([P, GROUPS, H], BF16)
-        w_words = keep.tile([P, 2 * H], U8, align_bytes=64)
-        w_scales = keep.tile([P, H], U8, align_bytes=64)
+        w_words = keep.tile([P, 2 * H], U8, align_bytes=MX_ALIGN)
+        w_scales = keep.tile([P, H], U8, align_bytes=MX_ALIGN)
 
         nc.vector.memset(w_scales[:].bitcast(I32), 0)
         ident = keep.tile([P, P], F32)
@@ -53,28 +60,32 @@ def tile_sindylossmixin_pa_s_kernel(
             nc.sync.dma_start(out=k2_sb[:, g, :], in_=k2_dram[:, :, g, :])
             nc.sync.dma_start(out=y_sb[:, g, :], in_=y_dram[:, :, g, :])
         nc.sync.dma_start(out=w_words[:].bitcast(I32), in_=coefficients_words[0].bitcast(I32))
-        for quadrant in range(4):
+        lower = slice(0, GROUPS // 2)
+        upper = slice(GROUPS // 2, GROUPS)
+        nc.sync.dma_start(out=k1_sb[:, lower, :], in_=k1_dram[:, :, lower, :])
+        for quadrant in range(QUADRANTS):
             nc.sync.dma_start(
-                out=w_scales[32 * quadrant : 32 * quadrant + 4, :].bitcast(I32),
-                in_=coefficients_scales[0, 4 * quadrant : 4 * quadrant + 4, :].bitcast(I32),
+                out=w_scales[QUADRANT * quadrant : QUADRANT * quadrant + LIVE_ROWS, :].bitcast(I32),
+                in_=coefficients_scales[
+                    0, LIVE_ROWS * quadrant : LIVE_ROWS * quadrant + LIVE_ROWS, :
+                ].bitcast(I32),
             )
-        for half in (slice(0, GROUPS // 2), slice(GROUPS // 2, GROUPS)):
-            nc.sync.dma_start(out=k1_sb[:, half, :], in_=k1_dram[:, :, half, :])
-        for half in (slice(0, GROUPS // 2), slice(GROUPS // 2, GROUPS)):
-            nc.sync.dma_start(out=next_sb[:, half, :], in_=next_dram[:, :, half, :])
+        nc.sync.dma_start(out=k1_sb[:, upper, :], in_=k1_dram[:, :, upper, :])
+        for two_groups in (lower, upper):
+            nc.sync.dma_start(out=next_sb[:, two_groups, :], in_=next_dram[:, :, two_groups, :])
 
         half_k2 = keep.tile([P, GROUPS, H], BF16)
-        stage_in = keep.tile([P, 2, GROUPS, H], BF16)
-        grouped = keep.tile([P, 2, GROUPS, P, 2], F32, align_bytes=64)
-        codes = keep.tile([P, 2, GROUPS, P], U32, align_bytes=64)
-        scales = keep.tile([P, 2, GROUPS, P], U8, align_bytes=64)
+        stage_in = keep.tile([P, STAGES, GROUPS, H], BF16)
+        grouped = keep.tile([P, STAGES, GROUPS, P, PAIRS], F32, align_bytes=MX_ALIGN)
+        codes = keep.tile([P, STAGES, GROUPS, P], U32, align_bytes=MX_ALIGN)
+        scales = keep.tile([P, STAGES, GROUPS, P], U8, align_bytes=MX_ALIGN)
         base = keep.tile([P, GROUPS, H], F32)
         result = keep.tile([P, GROUPS, H], F32)
 
         def turn_group(stage, g, bank):
             words = stage_in[:, stage, g, :].bitcast(F32)
-            for u in range(2):
-                nc.tensor.transpose(bank[:, u, :], words[:, u:WORDS:2], ident[:])
+            for u in range(PAIRS):
+                nc.tensor.transpose(bank[:, u, :], words[:, u:WORDS:PAIRS], ident[:])
             nc.scalar.copy(out=grouped[:, stage, g, :, :], in_=bank.rearrange("p u r -> p r u"))
 
         def quantise_group(stage, g):
@@ -122,13 +133,12 @@ def tile_sindylossmixin_pa_s_kernel(
             nc.vector.tensor_tensor(
                 out=stage_in[:, 0, g, :], in0=y_sb[:, g, :], in1=half_k2[:, g, :], op=ADD
             )
-            turned = psum.tile([P, 2, P], F32, tag="first")
+            turned = psum.tile([P, PAIRS, P], F32, tag="first")
             turn_group(0, g, turned)
 
         k3_banks = []
         sums = []
         for g in range(GROUPS):
-            base_step(g, k1_sb, 1.0 / 6.0)
             quantise_group(0, g)
             k3 = psum.tile([P, H], F32, tag="second")
             times_w(k3, 0, g, True, True)
@@ -136,19 +146,26 @@ def tile_sindylossmixin_pa_s_kernel(
             total = psum.tile([P, H], F32, tag="first")
             times_w(total, 0, g, True, False)
             sums.append(total)
+            base_step(g, k1_sb, 1.0 / 6.0)
+
+        for g in reversed(range(GROUPS // 2, GROUPS)):
+            nc.gpsimd.tensor_tensor(
+                out=base[:, g, :], in0=base[:, g, :], in1=next_sb[:, g, :], op=SUBTRACT
+            )
 
         for g in range(GROUPS):
             nc.vector.tensor_tensor(
                 out=stage_in[:, 1, g, :], in0=k3_banks[g][:], in1=y_sb[:, g, :], op=ADD
             )
-            turned = psum.tile([P, 2, P], F32, tag="second")
+            turned = psum.tile([P, PAIRS, P], F32, tag="second")
             turn_group(1, g, turned)
 
         for g in range(GROUPS):
-            base_step(g, next_sb, -1.0)
             times_w(sums[g], 0, g, False, False)
             quantise_group(1, g)
             times_w(sums[g], 1, g, False, True)
+            if g < GROUPS // 2:
+                base_step(g, next_sb, -1.0)
 
         for g in range(GROUPS):
             nc.vector.scalar_tensor_tensor(

@@ -85,7 +85,10 @@ def tile_sindylossmixin_pa_s_kernel(
         def turn_group(stage, g, bank):
             words = stage_in[:, stage, g, :].bitcast(F32)
             for u in range(PAIRS):
-                nc.tensor.transpose(bank[:, u, :], words[:, u:WORDS:PAIRS], ident[:])
+                if stage == 0:
+                    nc.tensor.transpose(bank[:, u, :], words[:, u:WORDS:PAIRS], ident[:])
+                else:
+                    nc.tensor.transpose(bank[:, u, :], words[:, u * P : (u + 1) * P], ident[:])
             nc.scalar.copy(out=grouped[:, stage, g, :, :], in_=bank.rearrange("p u r -> p r u"))
 
         def quantise_group(stage, g):
@@ -155,7 +158,10 @@ def tile_sindylossmixin_pa_s_kernel(
 
         for g in range(GROUPS):
             nc.vector.tensor_tensor(
-                out=stage_in[:, 1, g, :], in0=k3_banks[g][:], in1=y_sb[:, g, :], op=ADD
+                out=stage_in[:, 1, g, :].rearrange("p (u m e) -> p u m e", u=PAIRS, e=2),
+                in0=k3_banks[g][:].rearrange("p (m u e) -> p u m e", u=PAIRS, e=2),
+                in1=y_sb[:, g, :].rearrange("p (m u e) -> p u m e", u=PAIRS, e=2),
+                op=ADD,
             )
             turned = psum.tile([P, PAIRS, P], F32, tag="second")
             turn_group(1, g, turned)

@@ -48,7 +48,7 @@ def tile_sindylossmixin_pa_s_kernel(
         y_sb = keep.tile([P, GROUPS, H], BF16)
         k1_sb = keep.tile([P, GROUPS, H], BF16)
         k2_sb = keep.tile([P, GROUPS, H], BF16)
-        next_sb = keep.tile([P, GROUPS, H], BF16)
+        after_last = keep.tile([P, H], BF16)
         w_words = keep.tile([P, 2 * H], U8, align_bytes=MX_ALIGN)
         w_scales = keep.tile([P, H], U8, align_bytes=MX_ALIGN)
 
@@ -71,8 +71,7 @@ def tile_sindylossmixin_pa_s_kernel(
                 ].bitcast(I32),
             )
         nc.sync.dma_start(out=k1_sb[:, upper, :], in_=k1_dram[:, :, upper, :])
-        for two_groups in (lower, upper):
-            nc.sync.dma_start(out=next_sb[:, two_groups, :], in_=next_dram[:, :, two_groups, :])
+        nc.sync.dma_start(out=after_last[:], in_=next_dram[:, :, GROUPS - 1, :])
 
         half_k2 = keep.tile([P, GROUPS, H], BF16)
         stage_in = keep.tile([P, STAGES, GROUPS, H], BF16)
@@ -109,12 +108,12 @@ def tile_sindylossmixin_pa_s_kernel(
                 stop=stop,
             )
 
-        def base_step(g, in0, scalar):
+        def base_step(groups, in0, scalar):
             nc.vector.scalar_tensor_tensor(
-                out=base[:, g, :],
-                in0=in0[:, g, :],
+                out=base[:, groups, :],
+                in0=in0,
                 scalar=scalar,
-                in1=base[:, g, :],
+                in1=base[:, groups, :],
                 op0=MULT,
                 op1=ADD,
             )
@@ -124,7 +123,7 @@ def tile_sindylossmixin_pa_s_kernel(
         for g in range(GROUPS):
             nc.scalar.mul(out=half_k2[:, g, :], in_=k2_sb[:, g, :], mul=0.5)
 
-        for g in range(GROUPS):
+        def base_start(g):
             nc.vector.scalar_tensor_tensor(
                 out=base[:, g, :],
                 in0=k2_sb[:, g, :],
@@ -133,28 +132,45 @@ def tile_sindylossmixin_pa_s_kernel(
                 op0=MULT,
                 op1=ADD,
             )
+
+        def first_stage(g):
             nc.vector.tensor_tensor(
                 out=stage_in[:, 0, g, :], in0=y_sb[:, g, :], in1=half_k2[:, g, :], op=ADD
             )
             turned = psum.tile([P, PAIRS, P], F32, tag="first")
             turn_group(0, g, turned)
 
+        for g in range(GROUPS):
+            if g < GROUPS // 2:
+                base_start(g)
+                first_stage(g)
+            else:
+                first_stage(g)
+                base_start(g)
+
         k3_banks = []
         sums = []
-        for g in range(GROUPS):
-            quantise_group(0, g)
+
+        def k3_pass(g):
             k3 = psum.tile([P, H], F32, tag="second")
             times_w(k3, 0, g, True, True)
             k3_banks.append(k3)
+
+        def open_sum(g):
             total = psum.tile([P, H], F32, tag="first")
             times_w(total, 0, g, True, False)
             sums.append(total)
-            base_step(g, k1_sb, 1.0 / 6.0)
 
-        for g in reversed(range(GROUPS // 2, GROUPS)):
-            nc.gpsimd.tensor_tensor(
-                out=base[:, g, :], in0=base[:, g, :], in1=next_sb[:, g, :], op=SUBTRACT
-            )
+        for two_groups in (lower, upper):
+            for g in range(two_groups.start, two_groups.stop):
+                quantise_group(0, g)
+                k3_pass(g)
+                if g < GROUPS - 1:
+                    open_sum(g)
+            base_step(two_groups, k1_sb[:, two_groups, :], 1.0 / 6.0)
+
+        nc.gpsimd.tensor_tensor(out=base[:, 3, :], in0=base[:, 3, :], in1=after_last[:], op=SUBTRACT)
+        nc.gpsimd.tensor_tensor(out=base[:, 2, :], in0=base[:, 2, :], in1=y_sb[:, 3, :], op=SUBTRACT)
 
         for g in range(GROUPS):
             nc.vector.tensor_tensor(
@@ -165,13 +181,17 @@ def tile_sindylossmixin_pa_s_kernel(
             )
             turned = psum.tile([P, PAIRS, P], F32, tag="second")
             turn_group(1, g, turned)
+            if g == GROUPS // 2 - 1:
+                open_sum(GROUPS - 1)
+                times_w(sums[0], 0, 0, False, False)
 
         for g in range(GROUPS):
-            times_w(sums[g], 0, g, False, False)
+            if g > 0:
+                times_w(sums[g], 0, g, False, False)
             quantise_group(1, g)
             times_w(sums[g], 1, g, False, True)
-            if g < GROUPS // 2:
-                base_step(g, next_sb, -1.0)
+            if g == GROUPS // 2 - 1:
+                base_step(lower, y_sb[:, 1 : GROUPS // 2 + 1, :], -1.0)
 
         for g in range(GROUPS):
             nc.vector.scalar_tensor_tensor(

@@ -194,12 +194,16 @@ def tile_sindylossmixin_pa_s_kernel(
                 base_step(lower, y_sb[:, 1 : GROUPS // 2 + 1, :], -1.0)
 
         for g in range(GROUPS):
-            nc.vector.scalar_tensor_tensor(
-                out=result[:, g, :],
-                in0=sums[g][:],
-                scalar=1.0 / 6.0,
-                in1=base[:, g, :],
-                op0=MULT,
-                op1=ADD,
-            )
-            nc.sync.dma_start(out=out_dram[:, :, g, :], in_=result[:, g, :])
+            pieces = 2 if g == GROUPS - 1 else 1
+            width = H // pieces
+            for piece in range(pieces):
+                cols = slice(piece * width, (piece + 1) * width)
+                nc.vector.scalar_tensor_tensor(
+                    out=result[:, g, cols],
+                    in0=sums[g][:, cols],
+                    scalar=1.0 / 6.0,
+                    in1=base[:, g, cols],
+                    op0=MULT,
+                    op1=ADD,
+                )
+                nc.sync.dma_start(out=out_dram[:, :, g, cols], in_=result[:, g, cols])

@@ -167,9 +167,11 @@ def tile_sindylossmixin_pa_s_kernel(
                 k3_pass(g)
                 if g < GROUPS - 1:
                     open_sum(g)
-            base_step(two_groups, k1_sb[:, two_groups, :], 1.0 / 6.0)
+            if two_groups == lower:
+                base_step(lower, k1_sb[:, lower, :], 1.0 / 6.0)
+            else:
+                base_step(slice(2, 3), k1_sb[:, 2:3, :], 1.0 / 6.0)
 
-        nc.gpsimd.tensor_tensor(out=base[:, 3, :], in0=base[:, 3, :], in1=after_last[:], op=SUBTRACT)
         nc.gpsimd.tensor_tensor(out=base[:, 2, :], in0=base[:, 2, :], in1=y_sb[:, 3, :], op=SUBTRACT)
 
         for g in range(GROUPS):
@@ -192,6 +194,8 @@ def tile_sindylossmixin_pa_s_kernel(
             times_w(sums[g], 1, g, False, True)
             if g == GROUPS // 2 - 1:
                 base_step(lower, y_sb[:, 1 : GROUPS // 2 + 1, :], -1.0)
+        base_step(slice(3, 4), k1_sb[:, 3:4, :], 1.0 / 6.0)
+        nc.gpsimd.tensor_tensor(out=base[:, 3, :], in0=base[:, 3, :], in1=after_last[:], op=SUBTRACT)
 
         for g in range(GROUPS):
             pieces = 2 if g == GROUPS - 1 else 1

@@ -120,6 +120,14 @@ def tile_sindylossmixin_pa_s_kernel(
 
         ctx.enter_context(tc.manual_schedule())
 
+        idle_bank = psum.tile([P, P], F32, tag="second")
+
+        def keep_busy(times):
+            for again in range(times):
+                nc.tensor.matmul(idle_bank[:], lhsT=ident[:], rhs=ident[:], start=True, stop=True)
+
+        keep_busy(4)
+
         for g in range(GROUPS):
             nc.scalar.mul(out=half_k2[:, g, :], in_=k2_sb[:, g, :], mul=0.5)
 
@@ -139,6 +147,7 @@ def tile_sindylossmixin_pa_s_kernel(
             )
             turned = psum.tile([P, PAIRS, P], F32, tag="first")
             turn_group(0, g, turned)
+            keep_busy(1)
 
         for g in range(GROUPS):
             if g < GROUPS // 2:

@@ -20,6 +20,7 @@ SEQS = 8
 STEPS = 64
 GROUPS = 4
 STAGES = 2
+PACK = 4
 PAIRS = 2
 WORDS = H // 2
 QUADRANTS = 4
@@ -78,6 +79,8 @@ def tile_sindylossmixin_pa_s_kernel(
         grouped = keep.tile([P, STAGES, GROUPS, P, PAIRS], F32, align_bytes=MX_ALIGN)
         codes = keep.tile([P, STAGES, GROUPS, P], U32, align_bytes=MX_ALIGN)
         scales = keep.tile([P, STAGES, GROUPS, P], U8, align_bytes=MX_ALIGN)
+        y_wide = keep.tile([P, PACK, P], F32)
+        k3_wide = keep.tile([P, PACK, P], F32)
         base = keep.tile([P, GROUPS, H], F32)
         result = keep.tile([P, GROUPS, H], F32)
 
@@ -89,6 +92,34 @@ def tile_sindylossmixin_pa_s_kernel(
                 else:
                     nc.tensor.transpose(bank[:, u, :], words[:, u * P : (u + 1) * P], ident[:])
             nc.scalar.copy(out=grouped[:, stage, g, :, :], in_=bank.rearrange("p u r -> p r u"))
+
+        def widen_y(g):
+            nc.scalar.copy(
+                out=y_wide[:], in_=y_sb[:, g, :].rearrange("p (m t) -> p t m", t=PACK)
+            )
+
+        def take_k3(g):
+            nc.scalar.copy(
+                out=k3_wide[:], in_=k3_banks[g][:].rearrange("p (m t) -> p t m", t=PACK)
+            )
+
+        def turn_and_add(g, bank):
+            for t in range(PACK):
+                nc.tensor.matmul(
+                    bank[:, t, :], lhsT=y_wide[:, t, :], rhs=ident[:], is_transpose=True,
+                    start=True, stop=False,
+                )
+                nc.tensor.matmul(
+                    bank[:, t, :], lhsT=k3_wide[:, t, :], rhs=ident[:], is_transpose=True,
+                    start=False, stop=True,
+                )
+            nc.scalar.copy(
+                out=grouped[:, 1, g, :, :]
+                .rearrange("p r u -> p (r u)")
+                .bitcast(BF16)
+                .rearrange("p (r t) -> p r t", t=PACK),
+                in_=bank.rearrange("p t r -> p r t"),
+            )
 
         def quantise_group(stage, g):
             nc.vector.quantize_mx(
@@ -123,7 +154,7 @@ def tile_sindylossmixin_pa_s_kernel(
         idle_bank = psum.tile([P, P], F32, tag="second")
 
         def keep_busy(times):
-            for again in range(times):
+            for repeat in range(times):
                 nc.tensor.matmul(idle_bank[:], lhsT=ident[:], rhs=ident[:], start=True, stop=True)
 
         keep_busy(4)
@@ -153,6 +184,8 @@ def tile_sindylossmixin_pa_s_kernel(
             if g < GROUPS // 2:
                 base_start(g)
                 first_stage(g)
+                if g == 1:
+                    widen_y(0)
             else:
                 first_stage(g)
                 base_start(g)
@@ -174,16 +207,19 @@ def tile_sindylossmixin_pa_s_kernel(
             for g in range(two_groups.start, two_groups.stop):
                 quantise_group(0, g)
                 k3_pass(g)
-                if g < GROUPS - 1:
-                    open_sum(g)
             if two_groups == lower:
+                open_sum(0)
                 base_step(lower, k1_sb[:, lower, :], 1.0 / 6.0)
             else:
                 base_step(slice(2, 3), k1_sb[:, 2:3, :], 1.0 / 6.0)
 
         nc.gpsimd.tensor_tensor(out=base[:, 2, :], in0=base[:, 2, :], in1=y_sb[:, 3, :], op=SUBTRACT)
 
-        for g in range(GROUPS):
+        take_k3(0)
+        turned_sum = psum.tile([P, PACK, P], F32, tag="second")
+        turn_and_add(0, turned_sum)
+        open_sum(1)
+        for g in range(1, GROUPS):
             nc.vector.tensor_tensor(
                 out=stage_in[:, 1, g, :].rearrange("p (u m e) -> p u m e", u=PAIRS, e=2),
                 in0=k3_banks[g][:].rearrange("p (m u e) -> p u m e", u=PAIRS, e=2),
@@ -192,17 +228,15 @@ def tile_sindylossmixin_pa_s_kernel(
             )
             turned = psum.tile([P, PAIRS, P], F32, tag="second")
             turn_group(1, g, turned)
-            if g == GROUPS // 2 - 1:
-                open_sum(GROUPS - 1)
-                times_w(sums[0], 0, 0, False, False)
+            if g == 1:
+                open_sum(2)
+                open_sum(3)
+        base_step(lower, y_sb[:, 1 : GROUPS // 2 + 1, :], -1.0)
 
         for g in range(GROUPS):
-            if g > 0:
-                times_w(sums[g], 0, g, False, False)
+            times_w(sums[g], 0, g, False, False)
             quantise_group(1, g)
             times_w(sums[g], 1, g, False, True)
-            if g == GROUPS // 2 - 1:
-                base_step(lower, y_sb[:, 1 : GROUPS // 2 + 1, :], -1.0)
         base_step(slice(3, 4), k1_sb[:, 3:4, :], 1.0 / 6.0)
         nc.gpsimd.tensor_tensor(out=base[:, 3, :], in0=base[:, 3, :], in1=after_last[:], op=SUBTRACT)
 

@@ -237,8 +237,11 @@ def tile_sindylossmixin_pa_s_kernel(
             times_w(sums[g], 0, g, False, False)
             quantise_group(1, g)
             times_w(sums[g], 1, g, False, True)
-        base_step(slice(3, 4), k1_sb[:, 3:4, :], 1.0 / 6.0)
-        nc.gpsimd.tensor_tensor(out=base[:, 3, :], in0=base[:, 3, :], in1=after_last[:], op=SUBTRACT)
+            if g == 1:
+                base_step(slice(3, 4), k1_sb[:, 3:4, :], 1.0 / 6.0)
+                nc.gpsimd.tensor_tensor(
+                    out=base[:, 3, :], in0=base[:, 3, :], in1=after_last[:], op=SUBTRACT
+                )
 
         for g in range(GROUPS):
             pieces = 2 if g == GROUPS - 1 else 1

@@ -56,6 +56,13 @@ def tile_sindylossmixin_pa_s_kernel(
         nc.vector.memset(w_scales[:].bitcast(I32), 0)
         ident = keep.tile([P, P], F32)
         make_identity(nc, ident[:])
+        times_six = keep.tile([P, P], BF16)
+        times_two = keep.tile([P, P], BF16)
+        times_one = keep.tile([P, P], BF16)
+        for scaled, factor in ((times_six, 6.0), (times_two, 2.0), (times_one, 1.0)):
+            nc.gpsimd.tensor_scalar(
+                out=scaled[:], in0=ident[:], scalar1=factor, scalar2=0.0, op0=MULT, op1=ADD
+            )
 
         for g in range(GROUPS):
             nc.sync.dma_start(out=k2_sb[:, g, :], in_=k2_dram[:, :, g, :])
@@ -151,15 +158,12 @@ def tile_sindylossmixin_pa_s_kernel(
 
         ctx.enter_context(tc.manual_schedule())
 
-        idle_bank = psum.tile([P, P], F32, tag="second")
+        def halve_on_vector(g):
+            nc.vector.tensor_scalar(
+                out=half_k2[:, g, :], in0=k2_sb[:, g, :], scalar1=0.5, scalar2=None, op0=MULT
+            )
 
-        def keep_busy(times):
-            for repeat in range(times):
-                nc.tensor.matmul(idle_bank[:], lhsT=ident[:], rhs=ident[:], start=True, stop=True)
-
-        keep_busy(4)
-
-        for g in range(GROUPS):
+        for g in range(GROUPS // 2, GROUPS):
             nc.scalar.mul(out=half_k2[:, g, :], in_=k2_sb[:, g, :], mul=0.5)
 
         def base_start(g):
@@ -178,17 +182,27 @@ def tile_sindylossmixin_pa_s_kernel(
             )
             turned = psum.tile([P, PAIRS, P], F32, tag="first")
             turn_group(0, g, turned)
-            keep_busy(1)
 
-        for g in range(GROUPS):
-            if g < GROUPS // 2:
-                base_start(g)
-                first_stage(g)
-                if g == 1:
-                    widen_y(0)
-            else:
-                first_stage(g)
-                base_start(g)
+        plain_sum = psum.tile([P, H], F32, tag="second")
+
+        def add_plain(stationary, moving, start, stop):
+            nc.tensor.matmul(
+                plain_sum[:], lhsT=stationary[:], rhs=moving[:, 0, :], start=start, stop=stop
+            )
+
+        halve_on_vector(0)
+        first_stage(0)
+        add_plain(times_six, y_sb, True, False)
+        halve_on_vector(1)
+        first_stage(1)
+        widen_y(0)
+        add_plain(times_two, k2_sb, False, False)
+        base_start(1)
+        first_stage(2)
+        base_start(2)
+        first_stage(3)
+        base_start(3)
+        add_plain(times_one, k1_sb, False, True)
 
         k3_banks = []
         sums = []
@@ -203,22 +217,31 @@ def tile_sindylossmixin_pa_s_kernel(
             times_w(total, 0, g, True, False)
             sums.append(total)
 
-        for two_groups in (lower, upper):
-            for g in range(two_groups.start, two_groups.stop):
-                quantise_group(0, g)
-                k3_pass(g)
-            if two_groups == lower:
-                open_sum(0)
-                base_step(lower, k1_sb[:, lower, :], 1.0 / 6.0)
-            else:
-                base_step(slice(2, 3), k1_sb[:, 2:3, :], 1.0 / 6.0)
+        quantise_group(0, 0)
+        k3_pass(0)
+        quantise_group(0, 1)
+        k3_pass(1)
+        open_sum(0)
+        base_step(slice(1, 2), k1_sb[:, 1:2, :], 1.0 / 6.0)
+        quantise_group(0, 2)
+        k3_pass(2)
+        nc.vector.scalar_tensor_tensor(
+            out=base[:, 0, :],
+            in0=plain_sum[:],
+            scalar=1.0 / 6.0,
+            in1=y_sb[:, 1, :],
+            op0=MULT,
+            op1=SUBTRACT,
+        )
+        quantise_group(0, 3)
+        k3_pass(3)
+        base_step(slice(2, 3), k1_sb[:, 2:3, :], 1.0 / 6.0)
 
         nc.gpsimd.tensor_tensor(out=base[:, 2, :], in0=base[:, 2, :], in1=y_sb[:, 3, :], op=SUBTRACT)
 
         take_k3(0)
         turned_sum = psum.tile([P, PACK, P], F32, tag="second")
         turn_and_add(0, turned_sum)
-        open_sum(1)
         for g in range(1, GROUPS):
             nc.vector.tensor_tensor(
                 out=stage_in[:, 1, g, :].rearrange("p (u m e) -> p u m e", u=PAIRS, e=2),
@@ -229,9 +252,11 @@ def tile_sindylossmixin_pa_s_kernel(
             turned = psum.tile([P, PAIRS, P], F32, tag="second")
             turn_group(1, g, turned)
             if g == 1:
+                open_sum(1)
                 open_sum(2)
+            if g == GROUPS - 1:
                 open_sum(3)
-        base_step(lower, y_sb[:, 1 : GROUPS // 2 + 1, :], -1.0)
+        base_step(slice(1, 2), y_sb[:, 2:3, :], -1.0)
 
         for g in range(GROUPS):
             times_w(sums[g], 0, g, False, False)

@@ -94,10 +94,7 @@ def tile_sindylossmixin_pa_s_kernel(
         def turn_group(stage, g, bank):
             words = stage_in[:, stage, g, :].bitcast(F32)
             for u in range(PAIRS):
-                if stage == 0:
-                    nc.tensor.transpose(bank[:, u, :], words[:, u:WORDS:PAIRS], ident[:])
-                else:
-                    nc.tensor.transpose(bank[:, u, :], words[:, u * P : (u + 1) * P], ident[:])
+                nc.tensor.transpose(bank[:, u, :], words[:, u * P : (u + 1) * P], ident[:])
             nc.scalar.copy(out=grouped[:, stage, g, :, :], in_=bank.rearrange("p u r -> p r u"))
 
         def widen_y(g):
@@ -178,7 +175,10 @@ def tile_sindylossmixin_pa_s_kernel(
 
         def first_stage(g):
             nc.vector.tensor_tensor(
-                out=stage_in[:, 0, g, :], in0=y_sb[:, g, :], in1=half_k2[:, g, :], op=ADD
+                out=stage_in[:, 0, g, :].rearrange("p (u m e) -> p u m e", u=PAIRS, e=2),
+                in0=y_sb[:, g, :].rearrange("p (m u e) -> p u m e", u=PAIRS, e=2),
+                in1=half_k2[:, g, :].rearrange("p (m u e) -> p u m e", u=PAIRS, e=2),
+                op=ADD,
             )
             turned = psum.tile([P, PAIRS, P], F32, tag="first")
             turn_group(0, g, turned)
@@ -198,8 +198,8 @@ def tile_sindylossmixin_pa_s_kernel(
         widen_y(0)
         add_plain(times_two, k2_sb, False, False)
         base_start(1)
-        first_stage(2)
         base_start(2)
+        first_stage(2)
         first_stage(3)
         base_start(3)
         add_plain(times_one, k1_sb, False, True)
@@ -269,7 +269,7 @@ def tile_sindylossmixin_pa_s_kernel(
                 )
 
         for g in range(GROUPS):
-            pieces = 2 if g == GROUPS - 1 else 1
+            pieces = 2 if g in (0, GROUPS - 1) else 1
             width = H // pieces
             for piece in range(pieces):
                 cols = slice(piece * width, (piece + 1) * width)

@@ -192,10 +192,10 @@ def tile_sindylossmixin_pa_s_kernel(
 
         halve_on_vector(0)
         first_stage(0)
-        add_plain(times_six, y_sb, True, False)
         halve_on_vector(1)
         first_stage(1)
         widen_y(0)
+        add_plain(times_six, y_sb, True, False)
         add_plain(times_two, k2_sb, False, False)
         base_start(1)
         base_start(2)

@@ -143,12 +143,12 @@ def tile_sindylossmixin_pa_s_kernel(
                 stop=stop,
             )
 
-        def base_step(groups, in0, scalar):
+        def base_step(g, term, scalar, cols=slice(0, H)):
             nc.vector.scalar_tensor_tensor(
-                out=base[:, groups, :],
-                in0=in0,
+                out=base[:, g, cols],
+                in0=term[:, cols],
                 scalar=scalar,
-                in1=base[:, groups, :],
+                in1=base[:, g, cols],
                 op0=MULT,
                 op1=ADD,
             )
@@ -222,7 +222,7 @@ def tile_sindylossmixin_pa_s_kernel(
         quantise_group(0, 1)
         k3_pass(1)
         open_sum(0)
-        base_step(slice(1, 2), k1_sb[:, 1:2, :], 1.0 / 6.0)
+        base_step(1, k1_sb[:, 1, :], 1.0 / 6.0)
         quantise_group(0, 2)
         k3_pass(2)
         nc.vector.scalar_tensor_tensor(
@@ -235,7 +235,7 @@ def tile_sindylossmixin_pa_s_kernel(
         )
         quantise_group(0, 3)
         k3_pass(3)
-        base_step(slice(2, 3), k1_sb[:, 2:3, :], 1.0 / 6.0)
+        base_step(2, k1_sb[:, 2, :], 1.0 / 6.0)
 
         nc.gpsimd.tensor_tensor(out=base[:, 2, :], in0=base[:, 2, :], in1=y_sb[:, 3, :], op=SUBTRACT)
 
@@ -256,17 +256,16 @@ def tile_sindylossmixin_pa_s_kernel(
                 open_sum(2)
             if g == GROUPS - 1:
                 open_sum(3)
-        base_step(slice(1, 2), y_sb[:, 2:3, :], -1.0)
+        base_step(1, y_sb[:, 2, :], -1.0)
 
         for g in range(GROUPS):
             times_w(sums[g], 0, g, False, False)
             quantise_group(1, g)
             times_w(sums[g], 1, g, False, True)
             if g == 1:
-                base_step(slice(3, 4), k1_sb[:, 3:4, :], 1.0 / 6.0)
-                nc.gpsimd.tensor_tensor(
-                    out=base[:, 3, :], in0=base[:, 3, :], in1=after_last[:], op=SUBTRACT
-                )
+                base_step(3, k1_sb[:, 3, :], 1.0 / 6.0, slice(0, H // 2))
+        base_step(3, k1_sb[:, 3, :], 1.0 / 6.0, slice(H // 2, H))
+        nc.gpsimd.tensor_tensor(out=base[:, 3, :], in0=base[:, 3, :], in1=after_last[:], op=SUBTRACT)
 
         for g in range(GROUPS):
             pieces = 2 if g in (0, GROUPS - 1) else 1

@@ -67,7 +67,6 @@ def tile_sindylossmixin_pa_s_kernel(
         for g in range(GROUPS):
             nc.sync.dma_start(out=k2_sb[:, g, :], in_=k2_dram[:, :, g, :])
             nc.sync.dma_start(out=y_sb[:, g, :], in_=y_dram[:, :, g, :])
-        nc.sync.dma_start(out=w_words[:].bitcast(I32), in_=coefficients_words[0].bitcast(I32))
         lower = slice(0, GROUPS // 2)
         upper = slice(GROUPS // 2, GROUPS)
         nc.sync.dma_start(out=k1_sb[:, lower, :], in_=k1_dram[:, :, lower, :])
@@ -78,6 +77,7 @@ def tile_sindylossmixin_pa_s_kernel(
                     0, LIVE_ROWS * quadrant : LIVE_ROWS * quadrant + LIVE_ROWS, :
                 ].bitcast(I32),
             )
+        nc.sync.dma_start(out=w_words[:].bitcast(I32), in_=coefficients_words[0].bitcast(I32))
         nc.sync.dma_start(out=k1_sb[:, upper, :], in_=k1_dram[:, :, upper, :])
         nc.sync.dma_start(out=after_last[:], in_=next_dram[:, :, GROUPS - 1, :])
 

from contextlib import ExitStack

import concourse.mybir as mybir
from concourse.masks import make_identity

F32 = mybir.dt.float32
BF16 = mybir.dt.bfloat16
I32 = mybir.dt.int32
U32 = mybir.dt.uint32
U8 = mybir.dt.uint8
FP8X4 = mybir.dt.float8_e4m3fn_x4
FP4X4 = mybir.dt.float4_e2m1fn_x4
ADD = mybir.AluOpType.add
SUBTRACT = mybir.AluOpType.subtract
MULT = mybir.AluOpType.mult

P = 128
H = 512
SEQS = 8
STEPS = 64
GROUPS = 4
STAGES = 2
PACK = 4
PAIRS = 2
WORDS = H // 2
QUADRANTS = 4
QUADRANT = 32
LIVE_ROWS = 4
MX_ALIGN = 64

FLOPS = 2 * 2 * SEQS * STEPS * H * H


def tile_sindylossmixin_pa_s_kernel(
    tc, x, k1, k2, coefficients_words, coefficients_scales, out
):
    nc = tc.nc

    y_dram = x[:, 0:STEPS, :].rearrange("b (q g) h -> q b g h", g=GROUPS)
    next_dram = x[:, 1 : STEPS + 1, :].rearrange("b (q g) h -> q b g h", g=GROUPS)
    k1_dram = k1.rearrange("(b q g) h -> q b g h", b=SEQS, g=GROUPS)
    k2_dram = k2.rearrange("(b q g) h -> q b g h", b=SEQS, g=GROUPS)
    out_dram = out.rearrange("b (q g) h -> q b g h", g=GROUPS)

    with ExitStack() as ctx:
        keep = ctx.enter_context(tc.tile_pool(name="keep", bufs=1))
        psum = ctx.enter_context(tc.psum_pool(name="psum", bufs=GROUPS))

        y_sb = keep.tile([P, GROUPS, H], BF16)
        k1_sb = keep.tile([P, GROUPS, H], BF16)
        k2_sb = keep.tile([P, GROUPS, H], BF16)
        after_last = keep.tile([P, H], BF16)
        w_words = keep.tile([P, 2 * H], U8, align_bytes=MX_ALIGN)
        w_scales = keep.tile([P, H], U8, align_bytes=MX_ALIGN)

        nc.vector.memset(w_scales[:].bitcast(I32), 0)
        ident = keep.tile([P, P], F32)
        make_identity(nc, ident[:])
        times_six = keep.tile([P, P], BF16)
        times_two = keep.tile([P, P], BF16)
        times_one = keep.tile([P, P], BF16)
        for scaled, factor in ((times_six, 6.0), (times_two, 2.0), (times_one, 1.0)):
            nc.gpsimd.tensor_scalar(
                out=scaled[:], in0=ident[:], scalar1=factor, scalar2=0.0, op0=MULT, op1=ADD
            )

        for g in range(GROUPS):
            nc.sync.dma_start(out=k2_sb[:, g, :], in_=k2_dram[:, :, g, :])
            nc.sync.dma_start(out=y_sb[:, g, :], in_=y_dram[:, :, g, :])
        lower = slice(0, GROUPS // 2)
        upper = slice(GROUPS // 2, GROUPS)
        nc.sync.dma_start(out=k1_sb[:, lower, :], in_=k1_dram[:, :, lower, :])
        for quadrant in range(QUADRANTS):
            nc.sync.dma_start(
                out=w_scales[QUADRANT * quadrant : QUADRANT * quadrant + LIVE_ROWS, :].bitcast(I32),
                in_=coefficients_scales[
                    0, LIVE_ROWS * quadrant : LIVE_ROWS * quadrant + LIVE_ROWS, :
                ].bitcast(I32),
            )
        nc.sync.dma_start(out=w_words[:].bitcast(I32), in_=coefficients_words[0].bitcast(I32))
        nc.sync.dma_start(out=k1_sb[:, upper, :], in_=k1_dram[:, :, upper, :])
        nc.sync.dma_start(out=after_last[:], in_=next_dram[:, :, GROUPS - 1, :])

        half_k2 = keep.tile([P, GROUPS, H], BF16)
        stage_in = keep.tile([P, STAGES, GROUPS, H], BF16)
        grouped = keep.tile([P, STAGES, GROUPS, P, PAIRS], F32, align_bytes=MX_ALIGN)
        codes = keep.tile([P, STAGES, GROUPS, P], U32, align_bytes=MX_ALIGN)
        scales = keep.tile([P, STAGES, GROUPS, P], U8, align_bytes=MX_ALIGN)
        y_wide = keep.tile([P, PACK, P], F32)
        k3_wide = keep.tile([P, PACK, P], F32)
        base = keep.tile([P, GROUPS, H], F32)
        result = keep.tile([P, GROUPS, H], F32)

        def turn_group(stage, g, bank):
            words = stage_in[:, stage, g, :].bitcast(F32)
            for u in range(PAIRS):
                nc.tensor.transpose(bank[:, u, :], words[:, u * P : (u + 1) * P], ident[:])
            nc.scalar.copy(out=grouped[:, stage, g, :, :], in_=bank.rearrange("p u r -> p r u"))

        def widen_y(g):
            nc.scalar.copy(
                out=y_wide[:], in_=y_sb[:, g, :].rearrange("p (m t) -> p t m", t=PACK)
            )

        def take_k3(g):
            nc.scalar.copy(
                out=k3_wide[:], in_=k3_banks[g][:].rearrange("p (m t) -> p t m", t=PACK)
            )

        def turn_and_add(g, bank):
            for t in range(PACK):
                nc.tensor.matmul(
                    bank[:, t, :], lhsT=y_wide[:, t, :], rhs=ident[:], is_transpose=True,
                    start=True, stop=False,
                )
                nc.tensor.matmul(
                    bank[:, t, :], lhsT=k3_wide[:, t, :], rhs=ident[:], is_transpose=True,
                    start=False, stop=True,
                )
            nc.scalar.copy(
                out=grouped[:, 1, g, :, :]
                .rearrange("p r u -> p (r u)")
                .bitcast(BF16)
                .rearrange("p (r t) -> p r t", t=PACK),
                in_=bank.rearrange("p t r -> p r t"),
            )

        def quantise_group(stage, g):
            nc.vector.quantize_mx(
                out=codes[:, stage, g, :].bitcast(FP8X4),
                scales=scales[:, stage, g, :],
                in_=grouped[:, stage, g, :, :].rearrange("p r u -> p (r u)").bitcast(BF16),
            )

        def times_w(acc, stage, g, start, stop):
            nc.tensor.matmul_mx(
                out=acc[:],
                lhsT=codes[:, stage, g, :].bitcast(FP8X4),
                lhsT_scale=scales[:, stage, g, :],
                rhs=w_words[:].bitcast(FP4X4),
                rhs_scale=w_scales[:],
                start=start,
                stop=stop,
            )

        def base_step(g, term, scalar, cols=slice(0, H)):
            nc.vector.scalar_tensor_tensor(
                out=base[:, g, cols],
                in0=term[:, cols],
                scalar=scalar,
                in1=base[:, g, cols],
                op0=MULT,
                op1=ADD,
            )

        ctx.enter_context(tc.manual_schedule())

        def halve_on_vector(g):
            nc.vector.tensor_scalar(
                out=half_k2[:, g, :], in0=k2_sb[:, g, :], scalar1=0.5, scalar2=None, op0=MULT
            )

        for g in range(GROUPS // 2, GROUPS):
            nc.scalar.mul(out=half_k2[:, g, :], in_=k2_sb[:, g, :], mul=0.5)

        def base_start(g):
            nc.vector.scalar_tensor_tensor(
                out=base[:, g, :],
                in0=k2_sb[:, g, :],
                scalar=1.0 / 3.0,
                in1=y_sb[:, g, :],
                op0=MULT,
                op1=ADD,
            )

        def first_stage(g):
            nc.vector.tensor_tensor(
                out=stage_in[:, 0, g, :].rearrange("p (u m e) -> p u m e", u=PAIRS, e=2),
                in0=y_sb[:, g, :].rearrange("p (m u e) -> p u m e", u=PAIRS, e=2),
                in1=half_k2[:, g, :].rearrange("p (m u e) -> p u m e", u=PAIRS, e=2),
                op=ADD,
            )
            turned = psum.tile([P, PAIRS, P], F32, tag="first")
            turn_group(0, g, turned)

        plain_sum = psum.tile([P, H], F32, tag="second")

        def add_plain(stationary, moving, start, stop):
            nc.tensor.matmul(
                plain_sum[:], lhsT=stationary[:], rhs=moving[:, 0, :], start=start, stop=stop
            )

        halve_on_vector(0)
        first_stage(0)
        halve_on_vector(1)
        first_stage(1)
        widen_y(0)
        add_plain(times_six, y_sb, True, False)
        add_plain(times_two, k2_sb, False, False)
        base_start(1)
        base_start(2)
        first_stage(2)
        first_stage(3)
        base_start(3)
        add_plain(times_one, k1_sb, False, True)

        k3_banks = []
        sums = []

        def k3_pass(g):
            k3 = psum.tile([P, H], F32, tag="second")
            times_w(k3, 0, g, True, True)
            k3_banks.append(k3)

        def open_sum(g):
            total = psum.tile([P, H], F32, tag="first")
            times_w(total, 0, g, True, False)
            sums.append(total)

        quantise_group(0, 0)
        k3_pass(0)
        quantise_group(0, 1)
        k3_pass(1)
        open_sum(0)
        base_step(1, k1_sb[:, 1, :], 1.0 / 6.0)
        quantise_group(0, 2)
        k3_pass(2)
        nc.vector.scalar_tensor_tensor(
            out=base[:, 0, :],
            in0=plain_sum[:],
            scalar=1.0 / 6.0,
            in1=y_sb[:, 1, :],
            op0=MULT,
            op1=SUBTRACT,
        )
        quantise_group(0, 3)
        k3_pass(3)
        base_step(2, k1_sb[:, 2, :], 1.0 / 6.0)

        nc.gpsimd.tensor_tensor(out=base[:, 2, :], in0=base[:, 2, :], in1=y_sb[:, 3, :], op=SUBTRACT)

        take_k3(0)
        turned_sum = psum.tile([P, PACK, P], F32, tag="second")
        turn_and_add(0, turned_sum)
        for g in range(1, GROUPS):
            nc.vector.tensor_tensor(
                out=stage_in[:, 1, g, :].rearrange("p (u m e) -> p u m e", u=PAIRS, e=2),
                in0=k3_banks[g][:].rearrange("p (m u e) -> p u m e", u=PAIRS, e=2),
                in1=y_sb[:, g, :].rearrange("p (m u e) -> p u m e", u=PAIRS, e=2),
                op=ADD,
            )
            turned = psum.tile([P, PAIRS, P], F32, tag="second")
            turn_group(1, g, turned)
            if g == 1:
                open_sum(1)
                open_sum(2)
            if g == GROUPS - 1:
                open_sum(3)
        base_step(1, y_sb[:, 2, :], -1.0)

        for g in range(GROUPS):
            times_w(sums[g], 0, g, False, False)
            quantise_group(1, g)
            times_w(sums[g], 1, g, False, True)
            if g == 1:
                base_step(3, k1_sb[:, 3, :], 1.0 / 6.0, slice(0, H // 2))
        base_step(3, k1_sb[:, 3, :], 1.0 / 6.0, slice(H // 2, H))
        nc.gpsimd.tensor_tensor(out=base[:, 3, :], in0=base[:, 3, :], in1=after_last[:], op=SUBTRACT)

        for g in range(GROUPS):
            pieces = 2 if g in (0, GROUPS - 1) else 1
            width = H // pieces
            for piece in range(pieces):
                cols = slice(piece * width, (piece + 1) * width)
                nc.vector.scalar_tensor_tensor(
                    out=result[:, g, cols],
                    in0=sums[g][:, cols],
                    scalar=1.0 / 6.0,
                    in1=base[:, g, cols],
                    op0=MULT,
                    op1=ADD,
                )
                nc.sync.dma_start(out=out_dram[:, :, g, cols], in_=result[:, g, cols])
